import numpy as np
import ml_dtypes


def mxq(x, axis, fmt="e4m3"):
    dtype, down = {"e4m3": (ml_dtypes.float8_e4m3fn, 7), "e5m2": (ml_dtypes.float8_e5m2, 14)}[fmt]
    v = np.moveaxis(np.asarray(x, np.float32).astype(ml_dtypes.bfloat16).astype(np.float64), axis, -1)
    blocks = v.reshape(v.shape[:-1] + (-1, 32))
    amax = np.abs(blocks).max(-1, keepdims=True)
    byte = np.maximum(np.where(amax > 0, np.frexp(amax)[1] - 1 + 127, 0) - down, 1)
    scale = np.exp2(byte - 127.0)
    codes = (blocks / scale).astype(np.float32).astype(dtype).astype(np.float64)
    return np.moveaxis((codes * scale).reshape(v.shape), -1, axis)


WIDE = False


def mx_kscale(k):
    if not WIDE:
        return np.ones(k)
    levels = np.array([10, -10, 5, -5, 0])
    if k % 512:
        return np.exp2(np.random.permutation(np.resize(levels, k // 32))).repeat(32)
    a = np.empty((k // 512, 16))
    for p in range(k // 512):
        a[p, :8] = np.random.permutation(np.resize(levels, 8))
        for g in range(8):
            far = levels[np.abs(levels - a[p, g]) >= 10]
            a[p, g + 8] = far[np.random.randint(len(far))]
    return np.exp2(a.ravel()).repeat(32)


BF16 = ml_dtypes.bfloat16


def bf(x):
    return np.asarray(x, np.float32).astype(BF16)


def f64(x):
    return np.asarray(x).astype(np.float64)


E2M1 = np.array([0.0, 0.5, 1.0, 1.5, 2.0, 3.0, 4.0, 6.0, -0.0, -0.5, -1.0, -1.5, -2.0, -3.0, -4.0, -6.0])


def pack_weight(w, fmt):
    k, n = w.shape
    w = f64(bf(w)).reshape(k // 32, 32, n)
    amax = np.abs(w).max(1)
    if fmt == "e4m3":
        byte = np.frexp(amax)[1] - 1 + 127 - 7
    else:
        mant, ex = np.frexp(amax / 6.0)
        byte = np.where(mant > 0.5, ex, ex - 1) + 127
    byte = np.clip(np.where(amax > 0, byte, 1), 1, 254)
    scaled = (w * np.exp2(127.0 - byte)[:, None, :]).reshape(k, n).astype(np.float32)
    by_word = np.ascontiguousarray(scaled.reshape(k // 512, 128, 4, n).transpose(0, 1, 3, 2))
    if fmt == "e4m3":
        words = by_word.astype(ml_dtypes.float8_e4m3fn).view(np.uint8)
    else:
        c = by_word.astype(ml_dtypes.float4_e2m1fn).view(np.uint8) & 0xF
        words = c[..., 0::2] | (c[..., 1::2] << 4)
    return np.ascontiguousarray(words), np.ascontiguousarray(byte.astype(np.uint8).reshape(k // 512, 16, n))


def unpack_weight(words, scales, fmt):
    g, p, n, _ = words.shape
    if fmt == "e4m3":
        vals = np.ascontiguousarray(words).view(ml_dtypes.float8_e4m3fn).astype(np.float64)
    else:
        nib = np.empty((g, p, n, 4), np.uint8)
        nib[..., 0::2] = words & 0xF
        nib[..., 1::2] = words >> 4
        vals = E2M1[nib]
    vals = vals * np.repeat(np.exp2(scales.astype(np.float64) - 127.0), 8, axis=1)[..., None]
    return vals.transpose(0, 1, 3, 2).reshape(g * 512, n)


B, H, W, C, I, O, NH = 1, 2, 512, 512, 512, 512, 8
DH = I // NH
SCALE = DH ** -0.5


def draw0():
    s, t = mx_kscale(C), mx_kscale(I)
    sc = s[None, :, None, None]
    left_feat = bf(np.random.standard_normal((B, C, H, W)) * sc)
    right_feat = bf(np.random.standard_normal((B, C, H, W)) * sc)
    wq = np.random.standard_normal((I, C)) / np.sqrt(C) / s[None, :] * t[:, None]
    wk = np.random.standard_normal((I, C)) / np.sqrt(C) / s[None, :] / t[:, None]
    wq_words, wq_scales = pack_weight(wq.T, "e4m3")
    wk_words, wk_scales = pack_weight(wk.T, "e4m3")
    return {"left_feat": left_feat,
            "right_feat": right_feat,
            "wq_words": wq_words, "wq_scales": wq_scales,
            "wk_words": wk_words, "wk_scales": wk_scales}


def core(left_feat, right_feat, wq_words, wq_scales, wk_words, wk_scales):
    lf = f64(left_feat).reshape(B, C, H * W)
    rf = f64(right_feat).reshape(B, C, H * W)
    q = unpack_weight(wq_words, wq_scales, "e4m3").T @ mxq(lf, 1, "e4m3")
    k = unpack_weight(wk_words, wk_scales, "e4m3").T @ mxq(rf, 1, "e4m3")
    q = q.reshape(B, I, H, W).transpose(0, 2, 3, 1)
    k = k.reshape(B, I, H, W).transpose(0, 2, 1, 3)
    return (mxq(q, 3, "e4m3") @ mxq(k, 2, "e4m3")) * SCALE


def e4m3fn_bytes(y):
    return np.clip(np.asarray(y, np.float64), -448.0, 448.0).astype(np.float32).astype(ml_dtypes.float8_e4m3fn).view(np.uint8)


def e4m3fn_values(b):
    return np.asarray(b, np.uint8).view(ml_dtypes.float8_e4m3fn).astype(np.float64)


def setup_inputs():
    d = draw0()
    x0 = np.asarray(d['right_feat']).astype(np.float64)
    s = (np.max(np.abs(x0), axis=(0, 2, 3), keepdims=True) / 448.0).astype(np.float32)
    out = {}
    for k, v in d.items():
        if k == 'right_feat':
            out['right_feat_bytes'] = e4m3fn_bytes(x0 / s.astype(np.float64))
            out['right_feat_scale'] = s
        else:
            out[k] = v
    return out


def reference(left_feat, right_feat_bytes, right_feat_scale, wq_words, wq_scales, wk_words, wk_scales):
    return core(left_feat, e4m3fn_values(right_feat_bytes) * right_feat_scale.astype(np.float64), wq_words, wq_scales, wk_words, wk_scales)

@@ -1,0 +1,173 @@
+from contextlib import ExitStack
+
+import concourse.mybir as mybir
+from concourse.masks import make_identity
+
+F32 = mybir.dt.float32
+BF16 = mybir.dt.bfloat16
+I32 = mybir.dt.int32
+U32 = mybir.dt.uint32
+U8 = mybir.dt.uint8
+FP8 = mybir.dt.float8_e4m3fn
+FP8X4 = mybir.dt.float8_e4m3fn_x4
+COPY = mybir.ActivationFunctionType.Copy
+MULT = mybir.AluOpType.mult
+
+FLOPS = 4 * 512 * 512 * 1024 + 4 * 512 * 512 * 512
+
+ORDER = """
+W00:V W01:V W02:S W03:V LI00:P LI01:P LC00:S LC01:S IR00:V PK:V PSK:V XR00:V IR01:V KM00:P KM01:P KC00:S PSQ:V XR01:V KC01:S KM02:P KM03:P XL00:V PQ:V
+KC02:S XL01:V KC03:S QM00:P QM01:P W10:V W11:V LI10:P LI11:P QC00:S QC01:S QM02:P QM03:P W12:V W13:V QC02:S QC03:S IR10:V LC10:S LC11:S IR11:V XR10:V XK00:V
+KM10:P KM11:P XR11:V XL10:V XK01:V XL11:V KM12:P KM13:P XQ00:V XQ01:V KC10:S KC11:V KC12:S KC13:V D00:P D01:P QM10:P QM11:P QC10:S O00:V D02:P QC11:S XK10:V
+QM12:P QM13:P QC12:S O01:V QC13:S XK11:V XQ10:V D03:P O02:S XQ11:V D10:P D11:P O03:V O10:S D12:P O11:V D13:P O12:S O13:V
+""".split()
+
+
+def tile_sttm_single_pa_w8_kernel(tc, left_feat, right_bytes, right_scale, wq_words, wq_scales, wk_words, wk_scales, out):
+    nc = tc.nc
+    with ExitStack() as ctx:
+        sb = ctx.enter_context(tc.tile_pool(name="sb", bufs=1))
+        ps_li = ctx.enter_context(tc.psum_pool(name="ps_li", bufs=2))
+        ps_kq = ctx.enter_context(tc.psum_pool(name="ps_kq", bufs=3))
+        ps_o = ctx.enter_context(tc.psum_pool(name="ps_o", bufs=3))
+
+        def sbt(name, shape, dt):
+            return sb.tile(shape, dt, name=name, align_bytes=64)
+
+        rs = sbt("rs", [128, 4], F32)
+        rb = [sbt(f"rb{h}", [128, 4, 512], U8) for h in range(2)]
+        rw = [sbt(f"rw{h}", [128, 4, 512], BF16) for h in range(2)]
+        rg = [sbt(f"rg{h}", [128, 512, 4], BF16) for h in range(2)]
+        rc = [sbt(f"rc{h}", [128, 512], U32) for h in range(2)]
+        rq = [sbt(f"rq{h}", [128, 512], U8) for h in range(2)]
+        lr = [sbt(f"lr{h}", [128, 4, 512], BF16) for h in range(2)]
+        lg = [sbt(f"lg{h}", [128, 512, 4], BF16) for h in range(2)]
+        lc = [sbt(f"lc{h}", [128, 512], U32) for h in range(2)]
+        lq = [sbt(f"lq{h}", [128, 512], U8) for h in range(2)]
+        kg = [sbt(f"kg{h}", [128, 512, 4], BF16) for h in range(2)]
+        kc = [sbt(f"kc{h}", [128, 512], U32) for h in range(2)]
+        kq = [sbt(f"kq{h}", [128, 512], U8) for h in range(2)]
+        qg = [sbt(f"qg{h}", [128, 512, 4], BF16) for h in range(2)]
+        qc = [sbt(f"qc{h}", [128, 512], U32) for h in range(2)]
+        qq = [sbt(f"qq{h}", [128, 512], U8) for h in range(2)]
+        wraw = [sbt(f"wraw{w}", [128, 512], I32) for w in range(2)]
+        wprm = [sbt(f"wprm{w}", [128, 512], I32) for w in range(2)]
+        sraw = [sbt(f"sraw{w}", [128, 512], U8) for w in range(2)]
+        sprm = [sbt(f"sprm{w}", [128, 512], U8) for w in range(2)]
+        words = [wk_words, wq_words]
+        scales = [wk_scales, wq_scales]
+        osb = [[sbt(f"o{h}{b}", [128, 512], F32) for b in range(4)] for h in range(2)]
+        ident = sbt("ident", [128, 128], BF16)
+        one = sbt("one", [128, 1], F32)
+        one2 = sbt("one2", [128, 1], F32)
+
+        rview = right_bytes[0].rearrange("(p t) h x -> p t h x", t=4)
+        lview = left_feat[0].rearrange("(p t) h x -> p t h x", t=4)
+        live = {}
+
+        def load_r(h):
+            nc.sync.dma_start(out=rb[h][:], in_=rview[:, :, h, :])
+
+        def load_l(h):
+            nc.sync.dma_start(out=lr[h][:], in_=lview[:, :, h, :])
+
+        def load_w(w):
+            nc.sync.dma_start(out=wraw[w][:], in_=words[w][0].rearrange("p n t -> p (n t)").bitcast(I32))
+
+        def load_s(w):
+            for q in range(4):
+                nc.sync.dma_start(out=sraw[w][32 * q:32 * q + 4, :].bitcast(I32), in_=scales[w][0, 4 * q:4 * q + 4, :].bitcast(I32))
+
+        def permute(dst, src, i):
+            nc.vector.tensor_copy(out=dst.rearrange("p (t b i) -> p t b i", t=4, i=i), in_=src.rearrange("p (b t i) -> p t b i", t=4, i=i))
+
+        def empty(e, dst, src):
+            if e == "S":
+                nc.scalar.copy(out=dst, in_=src)
+            else:
+                nc.vector.tensor_copy(out=dst, in_=src)
+
+        def quant(codes, plane, src, j):
+            n = slice(256 * j, 256 * j + 256)
+            nc.vector.quantize_mx(out=codes[:, n].bitcast(FP8X4), scales=plane[:, n], in_=src[:, n, :].rearrange("p n t -> p (n t)"))
+
+        def project(w, codes, plane, b):
+            bank = ps_kq.tile([128, 4, 128], F32, name="kqbank")
+            n = slice(128 * b, 128 * b + 128)
+            for t in range(4):
+                m = slice(128 * t, 128 * t + 128)
+                nc.tensor.matmul_mx(out=bank[:, t, :], lhsT=wprm[w][:, m].bitcast(FP8X4), lhsT_scale=sprm[w][:, m], rhs=codes[:, n].bitcast(FP8X4), rhs_scale=plane[:, n], start=True, stop=True)
+            return bank
+
+        def step(name, e):
+            if name == "PK" or name == "PQ":
+                w = 0 if name == "PK" else 1
+                permute(wprm[w][:], wraw[w][:], 8)
+                return
+            if name == "PSK" or name == "PSQ":
+                w = 0 if name == "PSK" else 1
+                permute(sprm[w][:].bitcast(I32), sraw[w][:].bitcast(I32), 2)
+                return
+            kind, h, j = name[:-2], int(name[-2]), int(name[-1])
+            if kind == "W":
+                src = rb[h][:, j, :].bitcast(FP8)
+                if e == "S":
+                    nc.scalar.activation(out=rw[h][:, j, :], in_=src, func=COPY, scale=rs[:, j:j + 1])
+                else:
+                    nc.vector.tensor_scalar(out=rw[h][:, j, :], in0=src, scalar1=rs[:, j:j + 1], scalar2=None, op0=MULT)
+            elif kind == "IR":
+                n = slice(256 * j, 256 * j + 256)
+                nc.vector.tensor_copy(out=rg[h][:, n, :], in_=rw[h][:, :, n].rearrange("p t n -> p n t"))
+            elif kind == "XR":
+                quant(rc[h], rq[h], rg[h], j)
+            elif kind == "LI":
+                bank = ps_li.tile([128, 4, 256], BF16, name="libank")
+                for t in range(4):
+                    nc.tensor.matmul(bank[:, t, :], lhsT=ident[:], rhs=lr[h][:, t, 256 * j:256 * j + 256], start=True, stop=True)
+                live[name] = bank
+            elif kind == "LC":
+                empty(e, lg[h][:, 256 * j:256 * j + 256, :], live["LI" + name[-2:]][:].rearrange("p t n -> p n t"))
+            elif kind == "XL":
+                quant(lc[h], lq[h], lg[h], j)
+            elif kind == "KM":
+                live[name] = project(0, rc[h], rq[h], j)
+            elif kind == "QM":
+                live[name] = project(1, lc[h], lq[h], j)
+            elif kind == "KC":
+                empty(e, kg[h][:, 128 * j:128 * j + 128, :], live["KM" + name[-2:]][:].rearrange("p t n -> p n t"))
+            elif kind == "QC":
+                empty(e, qg[h][:, 128 * j:128 * j + 128, :], live["QM" + name[-2:]][:].rearrange("p t n -> p n t"))
+            elif kind == "XK":
+                quant(kc[h], kq[h], kg[h], j)
+            elif kind == "XQ":
+                quant(qc[h], qq[h], qg[h], j)
+            elif kind == "D":
+                bank = ps_o.tile([128, 512], F32, name="obank")
+                m = slice(128 * j, 128 * j + 128)
+                nc.tensor.matmul_mx(out=bank[:], lhsT=qc[h][:, m].bitcast(FP8X4), lhsT_scale=qq[h][:, m], rhs=kc[h][:].bitcast(FP8X4), rhs_scale=kq[h][:], start=True, stop=True)
+                live[name] = bank
+            elif kind == "O":
+                if e == "S":
+                    nc.scalar.activation(out=osb[h][j][:], in_=live["D" + name[-2:]][:], func=COPY, scale=0.125)
+                else:
+                    nc.vector.tensor_scalar(out=osb[h][j][:], in0=live["D" + name[-2:]][:], scalar1=0.125, scalar2=None, op0=MULT)
+                nc.sync.dma_start(out=out[0, h, 128 * j:128 * j + 128, :], in_=osb[h][j][:])
+
+        with tc.manual_schedule():
+            nc.vector.memset(one[:], 1.0)
+            nc.scalar.activation(out=one2[:], in_=one[:], func=COPY, scale=0.125)
+            for w in range(2):
+                nc.vector.memset(sraw[w][:].bitcast(I32), 0)
+            make_identity(nc, ident[:])
+            nc.sync.dma_start(out=rs[:], in_=right_scale.rearrange("o (p t) a b -> p (o t a b)", t=4))
+            load_r(0)
+            load_s(0)
+            load_l(0)
+            load_w(0)
+            load_w(1)
+            load_r(1)
+            load_s(1)
+            load_l(1)
+            for entry in ORDER:
+                name, engine = entry.split(":")
+                step(name, engine)

@@ -16,11 +16,14 @@ MULT = mybir.AluOpType.mult
 FLOPS = 4 * 512 * 512 * 1024 + 4 * 512 * 512 * 512
 
 ORDER = """
-W00:V W01:V W02:S W03:V LI00:P LI01:P LC00:S LC01:S IR00:V PK:V PSK:V XR00:V IR01:V KM00:P KM01:P KC00:S PSQ:V XR01:V KC01:S KM02:P KM03:P XL00:V PQ:V
-KC02:S XL01:V KC03:S QM00:P QM01:P W10:V W11:V LI10:P LI11:P QC00:S QC01:S QM02:P QM03:P W12:V W13:V QC02:S QC03:S IR10:V LC10:S LC11:S IR11:V XR10:V XK00:V
-KM10:P KM11:P XR11:V XL10:V XK01:V XL11:V KM12:P KM13:P XQ00:V XQ01:V KC10:S KC11:V KC12:S KC13:V D00:P D01:P QM10:P QM11:P QC10:S O00:V D02:P QC11:S XK10:V
-QM12:P QM13:P QC12:S O01:V QC13:S XK11:V XQ10:V D03:P O02:S XQ11:V D10:P D11:P O03:V O10:S D12:P O11:V D13:P O12:S O13:V
+W01:V W03:S W00:V W02:V W10:S RI01:P W11:S W12:V IR01:S LI01:P IR00:D W13:V RI10:P PK:V LC01:S LI10:P IR11:D PSK:V
+IR10:S XR11:V XR00:V KM12:P KM01:P XR01:V LC10:S XR10:V KC12:S KM13:P PQ:V KM11:P KC13:S LC11:D KM02:P PSQ:V XL11:V
+XL10:V KC01:S LC00:D XL01:V KM10:P XL00:V KC02:S QM10:P QC10:V QM11:P XK11:V KC11:S QM12:P QC12:V KC10:S KM03:P
+QM13:P QC11:S XQ10:V XK10:V QM02:P QC13:S KM00:P QC02:S XQ11:V QM03:P D10:P KC03:S KC00:V E13:P QC03:S O10:V D11:P
+QM01:P QM00:P XK00:V F13:S O11:S QC01:S E12:P XQ01:V XK01:V E11:P E10:P F11:S F10:S D02:P O02:S QC00:V F12:V XQ00:V
+D03:P D00:P O03:S O00:S D01:P O01:V
 """.split()
+LC_ENGINE = {entry[2:4]: entry[5] for entry in ORDER if entry.startswith("LC")}
 
 
 def tile_sttm_single_pa_w8_kernel(tc, left_feat, right_bytes, right_scale, wq_words, wq_scales, wk_words, wk_scales, out):
@@ -65,18 +68,24 @@ def tile_sttm_single_pa_w8_kernel(tc, left_feat, right_bytes, right_scale, wq_wo
         lview = left_feat[0].rearrange("(p t) h x -> p t h x", t=4)
         live = {}
 
-        def load_r(h):
-            nc.sync.dma_start(out=rb[h][:], in_=rview[:, :, h, :])
-
-        def load_l(h):
-            nc.sync.dma_start(out=lr[h][:], in_=lview[:, :, h, :])
-
-        def load_w(w):
-            nc.sync.dma_start(out=wraw[w][:], in_=words[w][0].rearrange("p n t -> p (n t)").bitcast(I32))
-
-        def load_s(w):
-            for q in range(4):
-                nc.sync.dma_start(out=sraw[w][32 * q:32 * q + 4, :].bitcast(I32), in_=scales[w][0, 4 * q:4 * q + 4, :].bitcast(I32))
+        def load(name):
+            if name == "R0":
+                nc.sync.dma_start(out=rb[0][:, 0:2, :], in_=rview[:, 0:2, 0, :])
+            elif name == "RB":
+                nc.sync.dma_start(out=rb[0][:, 2:4, :], in_=rview[:, 2:4, 0, :])
+            elif name == "R1":
+                nc.sync.dma_start(out=rb[1][:], in_=rview[:, :, 1, :])
+            elif name.startswith("L"):
+                h = int(name[1])
+                x = slice(256 * int(name[2]), 256 * int(name[2]) + 256) if len(name) == 3 else slice(0, 512)
+                nc.sync.dma_start(out=lr[h][:, :, x], in_=lview[:, :, h, x])
+            elif name.startswith("W"):
+                w = 0 if name == "WK" else 1
+                nc.sync.dma_start(out=wraw[w][:], in_=words[w][0].rearrange("p n t -> p (n t)").bitcast(I32))
+            else:
+                w = 0 if name == "KS" else 1
+                for q in range(4):
+                    nc.sync.dma_start(out=sraw[w][32 * q:32 * q + 4, :].bitcast(I32), in_=scales[w][0, 4 * q:4 * q + 4, :].bitcast(I32))
 
         def permute(dst, src, i):
             nc.vector.tensor_copy(out=dst.rearrange("p (t b i) -> p t b i", t=4, i=i), in_=src.rearrange("p (b t i) -> p t b i", t=4, i=i))
@@ -86,6 +95,16 @@ def tile_sttm_single_pa_w8_kernel(tc, left_feat, right_bytes, right_scale, wq_wo
                 nc.scalar.copy(out=dst, in_=src)
             else:
                 nc.vector.tensor_copy(out=dst, in_=src)
+
+        def direct(dst, src, n0):
+            n = slice(n0, n0 + 256)
+            nc.vector.tensor_copy(out=dst[:, n, :].rearrange("p (c i) t -> p c t i", i=4), in_=src[:, :, n].rearrange("p t (c i) -> p c t i", i=4))
+
+        def spread(src, n0):
+            bank = ps_li.tile([128, 256, 4], BF16, name="libank")
+            for i in range(0, 256, 128):
+                nc.tensor.matmul(bank[:, i:i + 128, :], lhsT=ident[:], rhs=src[:, :, n0 + i:n0 + i + 128].rearrange("p t n -> p n t"), start=True, stop=True)
+            return bank
 
         def quant(codes, plane, src, j):
             n = slice(256 * j, 256 * j + 256)
@@ -116,17 +135,22 @@ def tile_sttm_single_pa_w8_kernel(tc, left_feat, right_bytes, right_scale, wq_wo
                 else:
                     nc.vector.tensor_scalar(out=rw[h][:, j, :], in0=src, scalar1=rs[:, j:j + 1], scalar2=None, op0=MULT)
             elif kind == "IR":
-                n = slice(256 * j, 256 * j + 256)
-                nc.vector.tensor_copy(out=rg[h][:, n, :], in_=rw[h][:, :, n].rearrange("p t n -> p n t"))
+                if e == "D":
+                    direct(rg[h], rw[h], 256 * j)
+                else:
+                    empty(e, rg[h][:, 256 * j:256 * j + 256, :], live["RI" + name[-2:]][:])
             elif kind == "XR":
                 quant(rc[h], rq[h], rg[h], j)
             elif kind == "LI":
-                bank = ps_li.tile([128, 4, 256], BF16, name="libank")
-                for t in range(4):
-                    nc.tensor.matmul(bank[:, t, :], lhsT=ident[:], rhs=lr[h][:, t, 256 * j:256 * j + 256], start=True, stop=True)
-                live[name] = bank
+                if LC_ENGINE[name[-2:]] != "D":
+                    live[name] = spread(lr[h], 256 * j)
+            elif kind == "RI":
+                live[name] = spread(rw[h], 256 * j)
             elif kind == "LC":
-                empty(e, lg[h][:, 256 * j:256 * j + 256, :], live["LI" + name[-2:]][:].rearrange("p t n -> p n t"))
+                if e == "D":
+                    direct(lg[h], lr[h], 256 * j)
+                else:
+                    empty(e, lg[h][:, 256 * j:256 * j + 256, :], live["LI" + name[-2:]][:])
             elif kind == "XL":
                 quant(lc[h], lq[h], lg[h], j)
             elif kind == "KM":
@@ -146,6 +170,21 @@ def tile_sttm_single_pa_w8_kernel(tc, left_feat, right_bytes, right_scale, wq_wo
                 m = slice(128 * j, 128 * j + 128)
                 nc.tensor.matmul_mx(out=bank[:], lhsT=qc[h][:, m].bitcast(FP8X4), lhsT_scale=qq[h][:, m], rhs=kc[h][:].bitcast(FP8X4), rhs_scale=kq[h][:], start=True, stop=True)
                 live[name] = bank
+            elif kind == "E":
+                bank = ps_o.tile([128, 512], F32, name="obank")
+                b = 2 + j // 2
+                x = slice(256 * (j % 2), 256 * (j % 2) + 256)
+                m = slice(128 * b, 128 * b + 128)
+                nc.tensor.matmul_mx(out=bank[:, 0:256], lhsT=qc[h][:, m].bitcast(FP8X4), lhsT_scale=qq[h][:, m], rhs=kc[h][:, x].bitcast(FP8X4), rhs_scale=kq[h][:, x], start=True, stop=True)
+                live[name] = bank
+            elif kind == "F":
+                b = 2 + j // 2
+                x = slice(256 * (j % 2), 256 * (j % 2) + 256)
+                if e == "S":
+                    nc.scalar.activation(out=osb[h][b][:, x], in_=live["E" + name[-2:]][:, 0:256], func=COPY, scale=0.125)
+                else:
+                    nc.vector.tensor_scalar(out=osb[h][b][:, x], in0=live["E" + name[-2:]][:, 0:256], scalar1=0.125, scalar2=None, op0=MULT)
+                nc.sync.dma_start(out=out[0, h, 128 * b:128 * b + 128, x], in_=osb[h][b][:, x])
             elif kind == "O":
                 if e == "S":
                     nc.scalar.activation(out=osb[h][j][:], in_=live["D" + name[-2:]][:], func=COPY, scale=0.125)
@@ -160,14 +199,9 @@ def tile_sttm_single_pa_w8_kernel(tc, left_feat, right_bytes, right_scale, wq_wo
                 nc.vector.memset(sraw[w][:].bitcast(I32), 0)
             make_identity(nc, ident[:])
             nc.sync.dma_start(out=rs[:], in_=right_scale.rearrange("o (p t) a b -> p (o t a b)", t=4))
-            load_r(0)
-            load_s(0)
-            load_l(0)
-            load_w(0)
-            load_w(1)
-            load_r(1)
-            load_s(1)
-            load_l(1)
+
+            for item in "R0 RB R1 L01 WK L10 KS WQ L11 QS L00".split():
+                load(item)
             for entry in ORDER:
                 name, engine = entry.split(":")
                 step(name, engine)

@@ -1,7 +1,6 @@
 from contextlib import ExitStack
 
 import concourse.mybir as mybir
-from concourse.masks import make_identity
 
 F32 = mybir.dt.float32
 BF16 = mybir.dt.bfloat16
@@ -16,29 +15,27 @@ MULT = mybir.AluOpType.mult
 FLOPS = 4 * 512 * 512 * 1024 + 4 * 512 * 512 * 512
 
 ORDER = """
-W01:V W03:S W00:V W02:V W10:S RI01:P W11:S W12:V IR01:S LI01:P IR00:D W13:V RI10:P PK:V LC01:S LI10:P IR11:D PSK:V
-IR10:S XR11:V XR00:V KM12:P KM01:P XR01:V LC10:S XR10:V KC12:S KM13:P PQ:V KM11:P KC13:S LC11:D KM02:P PSQ:V XL11:V
-XL10:V KC01:S LC00:D XL01:V KM10:P XL00:V KC02:S QM10:P QC10:V QM11:P XK11:V KC11:S QM12:P QC12:V KC10:S KM03:P
-QM13:P QC11:S XQ10:V XK10:V QM02:P QC13:S KM00:P QC02:S XQ11:V QM03:P D10:P KC03:S KC00:V E13:P QC03:S O10:V D11:P
-QM01:P QM00:P XK00:V F13:S O11:S QC01:S E12:P XQ01:V XK01:V E11:P E10:P F11:S F10:S D02:P O02:S QC00:V F12:V XQ00:V
-D03:P D00:P O03:S O00:S D01:P O01:V
+W11:V W10:V W01:V W00:S W03:V W12:V W02:S W13:S IR00:V PK:V XR00:V PSK:V KM00:P IR11:S IR01:V XR11:V KM01:P XR01:V
+LC01:S LC00:V PQ:V KM12:P KC01:S XL01:V PSQ:V IR10:V LC10:V KM02:P KC12:S KC02:S XL00:V KM03:P KC00:S QM03:P QC03:S
+KM13:P QM02:P KC03:S QM00:P QC02:S XR10:V KM11:P KC13:S QM01:P KC11:S XL10:V XK01:V KM10:P XK00:V XQ01:V QC01:S
+QC00:V D02:P QM10:P D03:P XK11:V O02:S LC11:V XQ00:V QM11:P KC10:S QC10:S O03:S XL11:V QC11:V D00:P XK10:V XQ10:V
+D01:P QM13:P O00:S QC13:V O01:S QM12:P D10:P O10:S D11:P QC12:V O11:S XQ11:V E12:P E10:P F10:S E11:P E13:P F12:V
+F13:S F11:V
 """.split()
-LC_ENGINE = {entry[2:4]: entry[5] for entry in ORDER if entry.startswith("LC")}
 
 
 def tile_sttm_single_pa_w8_kernel(tc, left_feat, right_bytes, right_scale, wq_words, wq_scales, wk_words, wk_scales, out):
     nc = tc.nc
     with ExitStack() as ctx:
         sb = ctx.enter_context(tc.tile_pool(name="sb", bufs=1))
-        ps_li = ctx.enter_context(tc.psum_pool(name="ps_li", bufs=2))
-        ps_kq = ctx.enter_context(tc.psum_pool(name="ps_kq", bufs=3))
-        ps_o = ctx.enter_context(tc.psum_pool(name="ps_o", bufs=3))
+        ps_kq = ctx.enter_context(tc.psum_pool(name="ps_kq", bufs=4))
+        ps_o = ctx.enter_context(tc.psum_pool(name="ps_o", bufs=4))
 
         def sbt(name, shape, dt):
             return sb.tile(shape, dt, name=name, align_bytes=64)
 
         rs = sbt("rs", [128, 4], F32)
-        rb = [sbt(f"rb{h}", [128, 4, 512], U8) for h in range(2)]
+        rb = sbt("rb", [128, 4, 1024], U8)
         rw = [sbt(f"rw{h}", [128, 4, 512], BF16) for h in range(2)]
         rg = [sbt(f"rg{h}", [128, 512, 4], BF16) for h in range(2)]
         rc = [sbt(f"rc{h}", [128, 512], U32) for h in range(2)]
@@ -60,25 +57,21 @@ def tile_sttm_single_pa_w8_kernel(tc, left_feat, right_bytes, right_scale, wq_wo
         words = [wk_words, wq_words]
         scales = [wk_scales, wq_scales]
         osb = [[sbt(f"o{h}{b}", [128, 512], F32) for b in range(4)] for h in range(2)]
-        ident = sbt("ident", [128, 128], BF16)
         one = sbt("one", [128, 1], F32)
         one2 = sbt("one2", [128, 1], F32)
 
-        rview = right_bytes[0].rearrange("(p t) h x -> p t h x", t=4)
+        rview = right_bytes[0].rearrange("(p t) h x -> p t (h x)", t=4)
         lview = left_feat[0].rearrange("(p t) h x -> p t h x", t=4)
         live = {}
 
         def load(name):
-            if name == "R0":
-                nc.sync.dma_start(out=rb[0][:, 0:2, :], in_=rview[:, 0:2, 0, :])
+            if name == "RA":
+                nc.sync.dma_start(out=rb[:, 0:2, :], in_=rview[:, 0:2, :])
             elif name == "RB":
-                nc.sync.dma_start(out=rb[0][:, 2:4, :], in_=rview[:, 2:4, 0, :])
-            elif name == "R1":
-                nc.sync.dma_start(out=rb[1][:], in_=rview[:, :, 1, :])
+                nc.sync.dma_start(out=rb[:, 2:4, :], in_=rview[:, 2:4, :])
             elif name.startswith("L"):
                 h = int(name[1])
-                x = slice(256 * int(name[2]), 256 * int(name[2]) + 256) if len(name) == 3 else slice(0, 512)
-                nc.sync.dma_start(out=lr[h][:, :, x], in_=lview[:, :, h, x])
+                nc.sync.dma_start(out=lr[h][:], in_=lview[:, :, h, :])
             elif name.startswith("W"):
                 w = 0 if name == "WK" else 1
                 nc.sync.dma_start(out=wraw[w][:], in_=words[w][0].rearrange("p n t -> p (n t)").bitcast(I32))
@@ -96,15 +89,12 @@ def tile_sttm_single_pa_w8_kernel(tc, left_feat, right_bytes, right_scale, wq_wo
             else:
                 nc.vector.tensor_copy(out=dst, in_=src)
 
-        def direct(dst, src, n0):
+        def direct(e, dst, src, n0):
             n = slice(n0, n0 + 256)
-            nc.vector.tensor_copy(out=dst[:, n, :].rearrange("p (c i) t -> p c t i", i=4), in_=src[:, :, n].rearrange("p t (c i) -> p c t i", i=4))
-
-        def spread(src, n0):
-            bank = ps_li.tile([128, 256, 4], BF16, name="libank")
-            for i in range(0, 256, 128):
-                nc.tensor.matmul(bank[:, i:i + 128, :], lhsT=ident[:], rhs=src[:, :, n0 + i:n0 + i + 128].rearrange("p t n -> p n t"), start=True, stop=True)
-            return bank
+            if e == "S":
+                nc.scalar.copy(out=dst[:, n, :], in_=src[:, :, n].rearrange("p t n -> p n t"))
+            else:
+                nc.vector.tensor_copy(out=dst[:, n, :], in_=src[:, :, n].rearrange("p t n -> p n t"))
 
         def quant(codes, plane, src, j):
             n = slice(256 * j, 256 * j + 256)
@@ -129,28 +119,17 @@ def tile_sttm_single_pa_w8_kernel(tc, left_feat, right_bytes, right_scale, wq_wo
                 return
             kind, h, j = name[:-2], int(name[-2]), int(name[-1])
             if kind == "W":
-                src = rb[h][:, j, :].bitcast(FP8)
+                src = rb[:, j, 512 * h:512 * h + 512].bitcast(FP8)
                 if e == "S":
                     nc.scalar.activation(out=rw[h][:, j, :], in_=src, func=COPY, scale=rs[:, j:j + 1])
                 else:
                     nc.vector.tensor_scalar(out=rw[h][:, j, :], in0=src, scalar1=rs[:, j:j + 1], scalar2=None, op0=MULT)
             elif kind == "IR":
-                if e == "D":
-                    direct(rg[h], rw[h], 256 * j)
-                else:
-                    empty(e, rg[h][:, 256 * j:256 * j + 256, :], live["RI" + name[-2:]][:])
+                direct(e, rg[h], rw[h], 256 * j)
             elif kind == "XR":
                 quant(rc[h], rq[h], rg[h], j)
-            elif kind == "LI":
-                if LC_ENGINE[name[-2:]] != "D":
-                    live[name] = spread(lr[h], 256 * j)
-            elif kind == "RI":
-                live[name] = spread(rw[h], 256 * j)
             elif kind == "LC":
-                if e == "D":
-                    direct(lg[h], lr[h], 256 * j)
-                else:
-                    empty(e, lg[h][:, 256 * j:256 * j + 256, :], live["LI" + name[-2:]][:])
+                direct(e, lg[h], lr[h], 256 * j)
             elif kind == "XL":
                 quant(lc[h], lq[h], lg[h], j)
             elif kind == "KM":
@@ -197,10 +176,9 @@ def tile_sttm_single_pa_w8_kernel(tc, left_feat, right_bytes, right_scale, wq_wo
             nc.scalar.activation(out=one2[:], in_=one[:], func=COPY, scale=0.125)
             for w in range(2):
                 nc.vector.memset(sraw[w][:].bitcast(I32), 0)
-            make_identity(nc, ident[:])
             nc.sync.dma_start(out=rs[:], in_=right_scale.rearrange("o (p t) a b -> p (o t a b)", t=4))
 
-            for item in "R0 RB R1 L01 WK L10 KS WQ L11 QS L00".split():
+            for item in "RA RB WK L0 KS L1 WQ QS".split():
                 load(item)
             for entry in ORDER:
                 name, engine = entry.split(":")

@@ -92,9 +92,9 @@ def tile_sttm_single_pa_w8_kernel(tc, left_feat, right_bytes, right_scale, wq_wo
         def direct(e, dst, src, n0):
             n = slice(n0, n0 + 256)
             if e == "S":
-                nc.scalar.copy(out=dst[:, n, :], in_=src[:, :, n].rearrange("p t n -> p n t"))
+                nc.scalar.copy(out=dst[:, n, :].rearrange("p (c i) t -> p c t i", i=4), in_=src[:, :, n].rearrange("p t (c i) -> p c t i", i=4))
             else:
-                nc.vector.tensor_copy(out=dst[:, n, :], in_=src[:, :, n].rearrange("p t n -> p n t"))
+                nc.vector.tensor_copy(out=dst[:, n, :].rearrange("p (c i) t -> p c t i", i=4), in_=src[:, :, n].rearrange("p t (c i) -> p c t i", i=4))
 
         def quant(codes, plane, src, j):
             n = slice(256 * j, 256 * j + 256)

from contextlib import ExitStack

import concourse.mybir as mybir

F32 = mybir.dt.float32
BF16 = mybir.dt.bfloat16
I32 = mybir.dt.int32
U32 = mybir.dt.uint32
U8 = mybir.dt.uint8
FP8 = mybir.dt.float8_e4m3fn
FP8X4 = mybir.dt.float8_e4m3fn_x4
COPY = mybir.ActivationFunctionType.Copy
MULT = mybir.AluOpType.mult

FLOPS = 4 * 512 * 512 * 1024 + 4 * 512 * 512 * 512

ORDER = """
W11:V W10:V W01:V W00:S W03:V W12:V W02:S W13:S IR00:V PK:V XR00:V PSK:V KM00:P IR11:S IR01:V XR11:V KM01:P XR01:V
LC01:S LC00:V PQ:V KM12:P KC01:S XL01:V PSQ:V IR10:V LC10:V KM02:P KC12:S KC02:S XL00:V KM03:P KC00:S QM03:P QC03:S
KM13:P QM02:P KC03:S QM00:P QC02:S XR10:V KM11:P KC13:S QM01:P KC11:S XL10:V XK01:V KM10:P XK00:V XQ01:V QC01:S
QC00:V D02:P QM10:P D03:P XK11:V O02:S LC11:V XQ00:V QM11:P KC10:S QC10:S O03:S XL11:V QC11:V D00:P XK10:V XQ10:V
D01:P QM13:P O00:S QC13:V O01:S QM12:P D10:P O10:S D11:P QC12:V O11:S XQ11:V E12:P E10:P F10:S E11:P E13:P F12:V
F13:S F11:V
""".split()


def tile_sttm_single_pa_w8_kernel(tc, left_feat, right_bytes, right_scale, wq_words, wq_scales, wk_words, wk_scales, out):
    nc = tc.nc
    with ExitStack() as ctx:
        sb = ctx.enter_context(tc.tile_pool(name="sb", bufs=1))
        ps_kq = ctx.enter_context(tc.psum_pool(name="ps_kq", bufs=4))
        ps_o = ctx.enter_context(tc.psum_pool(name="ps_o", bufs=4))

        def sbt(name, shape, dt):
            return sb.tile(shape, dt, name=name, align_bytes=64)

        rs = sbt("rs", [128, 4], F32)
        rb = sbt("rb", [128, 4, 1024], U8)
        rw = [sbt(f"rw{h}", [128, 4, 512], BF16) for h in range(2)]
        rg = [sbt(f"rg{h}", [128, 512, 4], BF16) for h in range(2)]
        rc = [sbt(f"rc{h}", [128, 512], U32) for h in range(2)]
        rq = [sbt(f"rq{h}", [128, 512], U8) for h in range(2)]
        lr = [sbt(f"lr{h}", [128, 4, 512], BF16) for h in range(2)]
        lg = [sbt(f"lg{h}", [128, 512, 4], BF16) for h in range(2)]
        lc = [sbt(f"lc{h}", [128, 512], U32) for h in range(2)]
        lq = [sbt(f"lq{h}", [128, 512], U8) for h in range(2)]
        kg = [sbt(f"kg{h}", [128, 512, 4], BF16) for h in range(2)]
        kc = [sbt(f"kc{h}", [128, 512], U32) for h in range(2)]
        kq = [sbt(f"kq{h}", [128, 512], U8) for h in range(2)]
        qg = [sbt(f"qg{h}", [128, 512, 4], BF16) for h in range(2)]
        qc = [sbt(f"qc{h}", [128, 512], U32) for h in range(2)]
        qq = [sbt(f"qq{h}", [128, 512], U8) for h in range(2)]
        wraw = [sbt(f"wraw{w}", [128, 512], I32) for w in range(2)]
        wprm = [sbt(f"wprm{w}", [128, 512], I32) for w in range(2)]
        sraw = [sbt(f"sraw{w}", [128, 512], U8) for w in range(2)]
        sprm = [sbt(f"sprm{w}", [128, 512], U8) for w in range(2)]
        words = [wk_words, wq_words]
        scales = [wk_scales, wq_scales]
        osb = [[sbt(f"o{h}{b}", [128, 512], F32) for b in range(4)] for h in range(2)]
        one = sbt("one", [128, 1], F32)
        one2 = sbt("one2", [128, 1], F32)

        rview = right_bytes[0].rearrange("(p t) h x -> p t (h x)", t=4)
        lview = left_feat[0].rearrange("(p t) h x -> p t h x", t=4)
        live = {}

        def load(name):
            if name == "RA":
                nc.sync.dma_start(out=rb[:, 0:2, :], in_=rview[:, 0:2, :])
            elif name == "RB":
                nc.sync.dma_start(out=rb[:, 2:4, :], in_=rview[:, 2:4, :])
            elif name.startswith("L"):
                h = int(name[1])
                nc.sync.dma_start(out=lr[h][:], in_=lview[:, :, h, :])
            elif name.startswith("W"):
                w = 0 if name == "WK" else 1
                nc.sync.dma_start(out=wraw[w][:], in_=words[w][0].rearrange("p n t -> p (n t)").bitcast(I32))
            else:
                w = 0 if name == "KS" else 1
                for q in range(4):
                    nc.sync.dma_start(out=sraw[w][32 * q:32 * q + 4, :].bitcast(I32), in_=scales[w][0, 4 * q:4 * q + 4, :].bitcast(I32))

        def permute(dst, src, i):
            nc.vector.tensor_copy(out=dst.rearrange("p (t b i) -> p t b i", t=4, i=i), in_=src.rearrange("p (b t i) -> p t b i", t=4, i=i))

        def empty(e, dst, src):
            if e == "S":
                nc.scalar.copy(out=dst, in_=src)
            else:
                nc.vector.tensor_copy(out=dst, in_=src)

        def direct(e, dst, src, n0):
            n = slice(n0, n0 + 256)
            if e == "S":
                nc.scalar.copy(out=dst[:, n, :].rearrange("p (c i) t -> p c t i", i=4), in_=src[:, :, n].rearrange("p t (c i) -> p c t i", i=4))
            else:
                nc.vector.tensor_copy(out=dst[:, n, :].rearrange("p (c i) t -> p c t i", i=4), in_=src[:, :, n].rearrange("p t (c i) -> p c t i", i=4))

        def quant(codes, plane, src, j):
            n = slice(256 * j, 256 * j + 256)
            nc.vector.quantize_mx(out=codes[:, n].bitcast(FP8X4), scales=plane[:, n], in_=src[:, n, :].rearrange("p n t -> p (n t)"))

        def project(w, codes, plane, b):
            bank = ps_kq.tile([128, 4, 128], F32, name="kqbank")
            n = slice(128 * b, 128 * b + 128)
            for t in range(4):
                m = slice(128 * t, 128 * t + 128)
                nc.tensor.matmul_mx(out=bank[:, t, :], lhsT=wprm[w][:, m].bitcast(FP8X4), lhsT_scale=sprm[w][:, m], rhs=codes[:, n].bitcast(FP8X4), rhs_scale=plane[:, n], start=True, stop=True)
            return bank

        def step(name, e):
            if name == "PK" or name == "PQ":
                w = 0 if name == "PK" else 1
                permute(wprm[w][:], wraw[w][:], 8)
                return
            if name == "PSK" or name == "PSQ":
                w = 0 if name == "PSK" else 1
                permute(sprm[w][:].bitcast(I32), sraw[w][:].bitcast(I32), 2)
                return
            kind, h, j = name[:-2], int(name[-2]), int(name[-1])
            if kind == "W":
                src = rb[:, j, 512 * h:512 * h + 512].bitcast(FP8)
                if e == "S":
                    nc.scalar.activation(out=rw[h][:, j, :], in_=src, func=COPY, scale=rs[:, j:j + 1])
                else:
                    nc.vector.tensor_scalar(out=rw[h][:, j, :], in0=src, scalar1=rs[:, j:j + 1], scalar2=None, op0=MULT)
            elif kind == "IR":
                direct(e, rg[h], rw[h], 256 * j)
            elif kind == "XR":
                quant(rc[h], rq[h], rg[h], j)
            elif kind == "LC":
                direct(e, lg[h], lr[h], 256 * j)
            elif kind == "XL":
                quant(lc[h], lq[h], lg[h], j)
            elif kind == "KM":
                live[name] = project(0, rc[h], rq[h], j)
            elif kind == "QM":
                live[name] = project(1, lc[h], lq[h], j)
            elif kind == "KC":
                empty(e, kg[h][:, 128 * j:128 * j + 128, :], live["KM" + name[-2:]][:].rearrange("p t n -> p n t"))
            elif kind == "QC":
                empty(e, qg[h][:, 128 * j:128 * j + 128, :], live["QM" + name[-2:]][:].rearrange("p t n -> p n t"))
            elif kind == "XK":
                quant(kc[h], kq[h], kg[h], j)
            elif kind == "XQ":
                quant(qc[h], qq[h], qg[h], j)
            elif kind == "D":
                bank = ps_o.tile([128, 512], F32, name="obank")
                m = slice(128 * j, 128 * j + 128)
                nc.tensor.matmul_mx(out=bank[:], lhsT=qc[h][:, m].bitcast(FP8X4), lhsT_scale=qq[h][:, m], rhs=kc[h][:].bitcast(FP8X4), rhs_scale=kq[h][:], start=True, stop=True)
                live[name] = bank
            elif kind == "E":
                bank = ps_o.tile([128, 512], F32, name="obank")
                b = 2 + j // 2
                x = slice(256 * (j % 2), 256 * (j % 2) + 256)
                m = slice(128 * b, 128 * b + 128)
                nc.tensor.matmul_mx(out=bank[:, 0:256], lhsT=qc[h][:, m].bitcast(FP8X4), lhsT_scale=qq[h][:, m], rhs=kc[h][:, x].bitcast(FP8X4), rhs_scale=kq[h][:, x], start=True, stop=True)
                live[name] = bank
            elif kind == "F":
                b = 2 + j // 2
                x = slice(256 * (j % 2), 256 * (j % 2) + 256)
                if e == "S":
                    nc.scalar.activation(out=osb[h][b][:, x], in_=live["E" + name[-2:]][:, 0:256], func=COPY, scale=0.125)
                else:
                    nc.vector.tensor_scalar(out=osb[h][b][:, x], in0=live["E" + name[-2:]][:, 0:256], scalar1=0.125, scalar2=None, op0=MULT)
                nc.sync.dma_start(out=out[0, h, 128 * b:128 * b + 128, x], in_=osb[h][b][:, x])
            elif kind == "O":
                if e == "S":
                    nc.scalar.activation(out=osb[h][j][:], in_=live["D" + name[-2:]][:], func=COPY, scale=0.125)
                else:
                    nc.vector.tensor_scalar(out=osb[h][j][:], in0=live["D" + name[-2:]][:], scalar1=0.125, scalar2=None, op0=MULT)
                nc.sync.dma_start(out=out[0, h, 128 * j:128 * j + 128, :], in_=osb[h][j][:])

        with tc.manual_schedule():
            nc.vector.memset(one[:], 1.0)
            nc.scalar.activation(out=one2[:], in_=one[:], func=COPY, scale=0.125)
            for w in range(2):
                nc.vector.memset(sraw[w][:].bitcast(I32), 0)
            nc.sync.dma_start(out=rs[:], in_=right_scale.rearrange("o (p t) a b -> p (o t a b)", t=4))

            for item in "RA RB WK L0 KS L1 WQ QS".split():
                load(item)
            for entry in ORDER:
                name, engine = entry.split(":")
                step(name, engine)
